import numpy as np
import ml_dtypes


def mxq(x, axis, fmt="e4m3"):
    dtype, down = {"e4m3": (ml_dtypes.float8_e4m3fn, 7), "e5m2": (ml_dtypes.float8_e5m2, 14)}[fmt]
    v = np.moveaxis(np.asarray(x, np.float32).astype(ml_dtypes.bfloat16).astype(np.float64), axis, -1)
    blocks = v.reshape(v.shape[:-1] + (-1, 32))
    amax = np.abs(blocks).max(-1, keepdims=True)
    byte = np.maximum(np.where(amax > 0, np.frexp(amax)[1] - 1 + 127, 0) - down, 1)
    scale = np.exp2(byte - 127.0)
    codes = (blocks / scale).astype(np.float32).astype(dtype).astype(np.float64)
    return np.moveaxis((codes * scale).reshape(v.shape), -1, axis)


WIDE = False


def mx_kscale(k):
    if not WIDE:
        return np.ones(k)
    levels = np.array([10, -10, 5, -5, 0])
    a = np.random.permutation(np.resize(levels, k // 512 * 4)).reshape(k // 512, 4)
    idx = np.arange(k)
    return np.exp2(a[idx // 512, idx % 128 // 32])


BF16 = ml_dtypes.bfloat16


def bf(x):
    return np.asarray(x, np.float32).astype(BF16)


def f64(x):
    return np.asarray(x).astype(np.float64)


B, S, D, R, O = 4, 2048, 1024, 512, 256


def rfs(xw, dot_products, ab, AB):
    correction = (0.5 * np.sum(xw * xw, axis=-1))[..., None] * (ab * ab)
    return (1.0 / np.sqrt(R)) * AB * np.exp(dot_products - correction)


def setup_inputs():
    s = mx_kscale(D)
    s = s / s.max()
    return {"x": bf(np.random.standard_normal((B, S, D)) * 2.0 / np.sqrt(D) * s),
            "input_weights": bf(np.random.standard_normal((O, D)) * 2.0 / np.sqrt(D) * s),
            "xis": bf(np.random.uniform(size=R) * 0.5),
            "proj_matrix": bf(np.random.standard_normal((R, D)) / s)}


def reference(x, input_weights, xis, proj_matrix):
    x, input_weights, xis, proj_matrix = f64(x), f64(input_weights), f64(xis), f64(proj_matrix)
    ab = xis
    AB = np.exp(xis)
    gq = mxq(ab[:, None] * proj_matrix, 1, "e4m3")
    weights = rfs(input_weights, mxq(input_weights, 1, "e4m3") @ gq.T, ab, AB)
    feats = rfs(x, mxq(x, 2, "e4m3") @ gq.T, ab, AB)
    return mxq(feats, 2, "e4m3") @ mxq(weights, 1, "e4m3").T

@@ -1,0 +1,507 @@
+from contextlib import ExitStack
+
+import concourse.mybir as mybir
+from concourse.masks import make_identity
+
+F32 = mybir.dt.float32
+BF16 = mybir.dt.bfloat16
+U32 = mybir.dt.uint32
+U8 = mybir.dt.uint8
+FP8X4 = mybir.dt.float8_e4m3fn_x4
+ALU = mybir.AluOpType
+ACT = mybir.ActivationFunctionType
+
+P = 128
+D = 1024
+R = 512
+O = 256
+NTOK = 8192
+GROUP = 512
+NX = NTOK // GROUP
+NG = NX + 1
+FLOPS = 2 * (NTOK + O) * D * R + 2 * NTOK * R * O
+HALF_LN_R = 4.5 * 0.6931471805599453
+MANUAL = True
+XBUFS = 6
+TAIL_FROM = 14
+
+
+def norm_engine(s, j):
+    return "s"
+
+
+def copy_engine_out(s, h):
+    return "s" if (h == 1 or s >= 12) else "v"
+
+
+def copy_engine_x(s, b):
+    return "v"
+
+
+def copy_engine_nb(s):
+    return "v"
+
+
+def regroup_engine(s):
+    return "v" if s >= NG - 2 else "g"
+
+
+def tile_nnk_t_kernel(tc, x, input_weights, xis, proj_matrix, out):
+    nc = tc.nc
+    xf = x.flatten_outer_dims()
+    of = out.flatten_outer_dims()
+    with ExitStack() as ctx:
+        const = ctx.enter_context(tc.tile_pool(name="const", bufs=1))
+        xpool = ctx.enter_context(tc.tile_pool(name="xpool", bufs=XBUFS))
+        work = ctx.enter_context(tc.tile_pool(name="work", bufs=2))
+        small = ctx.enter_context(tc.tile_pool(name="small", bufs=4))
+        opool = ctx.enter_context(tc.tile_pool(name="opool", bufs=4))
+        ps_xt = ctx.enter_context(tc.psum_pool(name="ps_xt", bufs=2))
+        ps_d = ctx.enter_context(tc.psum_pool(name="ps_d", bufs=4))
+        ps_o = ctx.enter_context(tc.psum_pool(name="ps_o", bufs=1))
+        ps_n = ctx.enter_context(tc.psum_pool(name="ps_n", bufs=1))
+        single = ctx.enter_context(tc.tile_pool(name="single", bufs=1))
+        if MANUAL:
+            ctx.enter_context(tc.manual_schedule())
+
+        st = {}
+
+        def ntiles(s):
+            return 2 if s == 0 else 4
+
+        def valid(s):
+            return 0 <= s < NG
+
+        def psum_copy(eng, dst, src):
+            if eng == "v":
+                nc.vector.tensor_copy(out=dst, in_=src)
+            else:
+                nc.scalar.copy(out=dst, in_=src)
+
+        def load(s):
+            if not valid(s):
+                return
+            nt = ntiles(s)
+            xn = xpool.tile([P, nt, D], BF16, tag="xn", name="xn")
+            if s == 0:
+                src = input_weights.rearrange("(j p) k -> p j k", p=P)
+            else:
+                src = xf[(s - 1) * GROUP : s * GROUP, :].rearrange("(p j) k -> p j k", j=4)
+            nc.sync.dma_start(out=xn[:], in_=src)
+            st[("xn", s)] = xn
+
+        def load_w_tile(j):
+            nc.sync.dma_start(
+                out=st[("xn", 0)][:, j, :],
+                in_=input_weights.rearrange("(j p) k -> p j k", p=P)[:, j, :],
+            )
+
+        def load_proj_rows(t):
+            nc.sync.dma_start(
+                out=pj[:, t, :], in_=proj_matrix.rearrange("(p t) k -> p t k", t=4)[:, t, :]
+            )
+
+        xs_bf = const.tile([P, 4], BF16, name="xs_bf")
+        nc.sync.dma_start(out=xs_bf[:], in_=xis.rearrange("(p t) -> p t", t=4))
+        pj = const.tile([P, 4, D], BF16, name="pj")
+        xn_w = xpool.tile([P, 2, D], BF16, tag="xn", name="xn_w")
+        st[("xn", 0)] = xn_w
+        load_proj_rows(0)
+        load_proj_rows(1)
+        load_w_tile(0)
+        load_proj_rows(2)
+        load_proj_rows(3)
+        load_w_tile(1)
+        for s in range(1, 4):
+            load(s)
+
+        ident = const.tile([P, P], F32, name="ident")
+        make_identity(nc, ident[:])
+
+        warm_in = const.tile([P, 1], F32, name="warm_in")
+        warm_out = const.tile([P, 1], F32, name="warm_out")
+        nc.vector.memset(warm_in[:], 0.0)
+        nc.scalar.activation(out=warm_out[:], in_=warm_in[:], func=ACT.Exp)
+
+        xs = const.tile([P, 4], F32, name="xs")
+        nega = const.tile([P, 4], F32, name="nega")
+        bias = const.tile([P, 4], F32, name="bias")
+        nc.vector.tensor_copy(out=xs[:], in_=xs_bf[:])
+        nc.vector.scalar_tensor_tensor(
+            out=nega[:], in0=xs[:], scalar=-0.5, in1=xs[:], op0=ALU.mult, op1=ALU.mult
+        )
+        nc.vector.tensor_scalar_add(out=bias[:], in0=xs[:], scalar1=-HALF_LN_R)
+
+        junks = const.tile([P, D], BF16, name="junks")
+
+        xb_ps = ps_n.tile([P, 4, P], F32, tag="nbp", name="xb_ps")
+        for t in range(4):
+            nc.tensor.transpose(xb_ps[:, t, :], xs[:, t : t + 1].to_broadcast([P, P]), ident[:])
+        xisb = const.tile([P, 4, P], F32, name="xisb")
+        nc.vector.tensor_copy(out=xisb[:], in_=xb_ps[:])
+
+        gg = const.tile([P, 2, R, 4], BF16, name="gg", align_bytes=64)
+        gc = const.tile([P, 2, R], U32, name="gc", align_bytes=64)
+        gsc = const.tile([P, 2, R], U8, name="gsc", align_bytes=64)
+        pjw = pj[:].bitcast(F32)
+
+        def g_transposes(h, g):
+            pg = ps_d.tile([P, 2, 2, P], F32, tag="d", name="pg")
+            for tt in range(2):
+                for u in range(2):
+                    w0 = 256 * g + 128 * u
+                    nc.tensor.transpose(pg[:, tt, u, :], pjw[:, 2 * h + tt, w0 : w0 + P], ident[:])
+            st[("pg", h, g)] = pg
+
+        def g_multiply(h, g):
+            pg = st[("pg", h, g)]
+            for tt in range(2):
+                tp = 2 * h + tt
+                nc.vector.tensor_tensor(
+                    out=gg[:, g, tp * P : (tp + 1) * P, :].rearrange("p q (u e) -> p q u e", e=2),
+                    in0=pg[:, tt].bitcast(BF16).rearrange("p u (q e) -> p q u e", e=2),
+                    in1=xisb[:, tp, :].unsqueeze(2).unsqueeze(3).to_broadcast([P, P, 2, 2]),
+                    op=ALU.mult,
+                )
+
+        def quant_g():
+            nc.vector.quantize_mx(
+                out=gc[:].rearrange("p g n -> p (g n)").bitcast(FP8X4),
+                scales=gsc[:].rearrange("p g n -> p (g n)"),
+                in_=gg[:].rearrange("p g n t -> p (g n t)"),
+            )
+
+        wc = const.tile([P, O], U32, name="wc", align_bytes=64)
+        wsc = const.tile([P, O], U8, name="wsc", align_bytes=64)
+
+        def norm_col(s, j):
+            return st[("n" + norm_engine(s, j), s)][:, j : j + 1]
+
+        def norm(s, j):
+            if not valid(s) or j >= ntiles(s):
+                return
+            eng = norm_engine(s, j)
+            if ("n" + eng, s) not in st:
+                ncols = small.tile([P, 4], F32, tag="n" + eng, name="ncols")
+                st[("n" + eng, s)] = ncols
+            xn = st[("xn", s)]
+            nc.scalar.activation(
+                out=junks[:], in_=xn[:, j, :], func=ACT.Square, accum_out=norm_col(s, j)
+            )
+
+        def banks(s):
+            return [(g, h) for h in range(ntiles(s) // 2) for g in range(2)]
+
+        def xt(s, bs):
+            if not valid(s):
+                return
+            xw = st[("xn", s)][:].bitcast(F32)
+            for b in bs:
+                if b >= len(banks(s)):
+                    continue
+                g, h = banks(s)[b]
+                xtp = ps_xt.tile([P, 2, 2, P], F32, tag="xt", name="xtp")
+                for u in range(2):
+                    for jj in range(2):
+                        w0 = 256 * g + 128 * u
+                        nc.tensor.transpose(xtp[:, u, jj, :], xw[:, 2 * h + jj, w0 : w0 + P], ident[:])
+                st[("xt", s, b)] = xtp
+
+        def xo(s, b):
+            if not valid(s) or b >= len(banks(s)):
+                return
+            if b == 0:
+                xg = work.tile([P, 2, ntiles(s) * P, 4], BF16, tag="xg", name="xg", align_bytes=64)
+                st[("xg", s)] = xg
+            xg32 = st[("xg", s)][:].bitcast(F32)
+            g, h = banks(s)[b]
+            psum_copy(
+                copy_engine_x(s, b),
+                xg32[:, g, h * 256 : (h + 1) * 256, :],
+                st[("xt", s, b)][:].rearrange("p u j c -> p (j c) u"),
+            )
+
+        def quant_x(s):
+            if not valid(s):
+                return
+            n = ntiles(s) * P
+            xc = work.tile([P, 2, n], U32, tag="xc", name="xc", align_bytes=64)
+            xsc = work.tile([P, 2, n], U8, tag="xsc", name="xsc", align_bytes=64)
+            nc.vector.quantize_mx(
+                out=xc[:].rearrange("p g n -> p (g n)").bitcast(FP8X4),
+                scales=xsc[:].rearrange("p g n -> p (g n)"),
+                in_=st[("xg", s)][:].rearrange("p g n t -> p (g n t)"),
+            )
+            st[("xc", s)] = xc
+            st[("xsc", s)] = xsc
+
+        def nb_pe(s):
+            if not valid(s):
+                return
+            nt = ntiles(s)
+            nbp = ps_n.tile([P, nt, P], F32, tag="nbp", name="nbp")
+            for j in range(nt):
+                nc.tensor.transpose(nbp[:, j, :], norm_col(s, j).to_broadcast([P, P]), ident[:])
+            st[("nbp", s)] = nbp
+
+        def nb_copy(s):
+            if not valid(s):
+                return
+            nt = ntiles(s)
+            nb = work.tile([P, nt * P], F32, tag="nb", name="nb")
+            psum_copy(copy_engine_nb(s), nb[:], st[("nbp", s)][:].rearrange("p j c -> p (j c)"))
+            st[("nb", s)] = nb
+
+        def mx1(s, t):
+            if not valid(s):
+                return
+            n = ntiles(s) * P
+            xc = st[("xc", s)]
+            xsc = st[("xsc", s)]
+            d = ps_d.tile([P, n], F32, tag="d", name="d")
+            for g in range(2):
+                nc.tensor.matmul_mx(
+                    out=d[:],
+                    lhsT=gc[:, g, t * P : (t + 1) * P].bitcast(FP8X4),
+                    lhsT_scale=gsc[:, g, t * P : (t + 1) * P],
+                    rhs=xc[:, g, :].bitcast(FP8X4),
+                    rhs_scale=xsc[:, g, :],
+                    start=(g == 0),
+                    stop=(g == 1),
+                )
+            st[("d", s, t)] = d
+
+        def stt(s, t):
+            if not valid(s):
+                return
+            n = ntiles(s) * P
+            if t == 0:
+                z = work.tile([P, 4, n], F32, tag="z", name="z")
+                st[("z", s)] = z
+            nc.vector.scalar_tensor_tensor(
+                out=st[("z", s)][:, t, :],
+                in0=st[("nb", s)][:],
+                scalar=nega[:, t : t + 1],
+                in1=st[("d", s, t)][:],
+                op0=ALU.mult,
+                op1=ALU.add,
+            )
+
+        def expo(s, t):
+            if not valid(s):
+                return
+            n = ntiles(s) * P
+            if t == 0:
+                f = work.tile([P, 4, n], BF16, tag="f", name="f")
+                st[("f", s)] = f
+            nc.scalar.activation(
+                out=st[("f", s)][:, t, :],
+                in_=st[("z", s)][:, t, :],
+                func=ACT.Exp,
+                bias=bias[:, t : t + 1],
+                scale=1.0,
+            )
+
+        def regroup(s):
+            if not valid(s):
+                return
+            n = ntiles(s) * P
+            fg = single.tile([P, n, 4], BF16, tag="fg", name="fg", align_bytes=64)
+            if regroup_engine(s) == "v":
+                nc.vector.tensor_copy(
+                    out=fg[:].rearrange("p (c i) t -> p c t i", i=4),
+                    in_=st[("f", s)][:].rearrange("p t (c i) -> p c t i", i=4),
+                )
+            else:
+                nc.gpsimd.tensor_scalar(
+                    out=fg[:],
+                    in0=st[("f", s)][:].rearrange("p t n -> p n t"),
+                    scalar1=1.0,
+                    scalar2=0.0,
+                    op0=ALU.mult,
+                    op1=ALU.add,
+                )
+            st[("fg", s)] = fg
+
+        def quant_f(s):
+            if not valid(s):
+                return
+            n = ntiles(s) * P
+            if s == 0:
+                fc = wc
+                fsc = wsc
+            else:
+                fc = work.tile([P, n], U32, tag="fc", name="fc", align_bytes=64)
+                fsc = work.tile([P, n], U8, tag="fsc", name="fsc", align_bytes=64)
+            nc.vector.quantize_mx(
+                out=fc[:].bitcast(FP8X4),
+                scales=fsc[:],
+                in_=st[("fg", s)][:].rearrange("p n t -> p (n t)"),
+            )
+            st[("fc", s)] = fc
+            st[("fsc", s)] = fsc
+
+        def mx2(s, h):
+            if not (1 <= s < NG):
+                return
+            fc = st[("fc", s)]
+            fsc = st[("fsc", s)]
+            if s >= TAIL_FROM:
+                o = ps_d.tile([P, 2, O], F32, tag="d", name="o")
+            else:
+                o = ps_o.tile([P, 2, O], F32, tag="o", name="o")
+            for jj in range(2):
+                j = 2 * h + jj
+                nc.tensor.matmul_mx(
+                    out=o[:, jj, :],
+                    lhsT=fc[:, j * P : (j + 1) * P].bitcast(FP8X4),
+                    lhsT_scale=fsc[:, j * P : (j + 1) * P],
+                    rhs=wc[:].bitcast(FP8X4),
+                    rhs_scale=wsc[:],
+                    start=True,
+                    stop=True,
+                )
+            st[("o", s, h)] = o
+
+        def out_copy(s, h):
+            if not (1 <= s < NG):
+                return
+            if h == 0:
+                osb = opool.tile([P, 4, O], F32, tag="osb", name="osb")
+                st[("osb", s)] = osb
+            osb = st[("osb", s)]
+            psum_copy(copy_engine_out(s, h), osb[:, 2 * h : 2 * h + 2, :], st[("o", s, h)][:])
+            dst = of[(s - 1) * GROUP : s * GROUP, :].rearrange("(p j) o -> p j o", j=4)
+            if s == NG - 1:
+                nc.sync.dma_start(out=dst[:, 2 * h : 2 * h + 2, :], in_=osb[:, 2 * h : 2 * h + 2, :])
+            elif h == 1:
+                nc.sync.dma_start(out=dst, in_=osb[:])
+
+        g_transposes(0, 0)
+        g_transposes(0, 1)
+        g_multiply(0, 0)
+        g_multiply(0, 1)
+        norm(0, 0)
+        norm(0, 1)
+        xt(0, [0, 1])
+        xo(0, 0)
+        xo(0, 1)
+        g_transposes(1, 0)
+        g_transposes(1, 1)
+        g_multiply(1, 0)
+        g_multiply(1, 1)
+        load(4)
+        for j in range(4):
+            norm(1, j)
+        xt(1, [0, 1])
+        xo(1, 0)
+        xo(1, 1)
+        quant_g()
+        quant_x(0)
+        xt(1, [2, 3])
+        load(5)
+        xo(1, 2)
+        xo(1, 3)
+        nb_pe(0)
+        nb_copy(0)
+        quant_x(1)
+        for j in range(4):
+            norm(2, j)
+        xt(2, [0, 1])
+        for t in range(4):
+            mx1(0, t)
+        nb_pe(1)
+        load(6)
+        xo(2, 0)
+        xo(2, 1)
+        for t in range(4):
+            stt(0, t)
+        expo(0, 0)
+        norm(3, 0)
+        norm(3, 1)
+        expo(0, 1)
+        expo(0, 2)
+        expo(0, 3)
+        norm(3, 2)
+        xt(2, [2, 3])
+        xo(2, 2)
+        xo(2, 3)
+        for t in range(4):
+            mx1(1, t)
+        nb_copy(1)
+        quant_x(2)
+        xt(3, [0, 1])
+        nb_pe(2)
+        load(7)
+
+        for i in range(1, NG - 2):
+            quant_f(i - 2)
+            out_copy(i - 3, 1)
+            stt(i, 0)
+            norm(i + 2, 3)
+            xo(i + 2, 0)
+            regroup(i - 1)
+            xo(i + 2, 1)
+            load(i + 7)
+            expo(i, 0)
+            stt(i, 1)
+            xt(i + 2, [2, 3])
+            norm(i + 3, 0)
+            stt(i, 2)
+            mx1(i + 1, 0)
+            stt(i, 3)
+            mx2(i - 2, 0)
+            norm(i + 3, 1)
+            xo(i + 2, 2)
+            mx1(i + 1, 1)
+            xo(i + 2, 3)
+            mx1(i + 1, 2)
+            expo(i, 1)
+            nb_copy(i + 1)
+            mx1(i + 1, 3)
+            expo(i, 2)
+            expo(i, 3)
+            out_copy(i - 2, 0)
+            xt(i + 3, [0, 1])
+            quant_x(i + 2)
+            nb_pe(i + 2)
+            norm(i + 3, 2)
+            mx2(i - 2, 1)
+
+        quant_f(13)
+        out_copy(12, 1)
+        regroup(14)
+        for t in range(4):
+            stt(15, t)
+        for t in range(4):
+            expo(15, t)
+        mx1(16, 0)
+        mx2(13, 0)
+        mx1(16, 1)
+        mx1(16, 2)
+        mx1(16, 3)
+        nb_copy(16)
+        out_copy(13, 0)
+        mx2(13, 1)
+        for t in range(4):
+            stt(16, t)
+        for t in range(4):
+            expo(16, t)
+        out_copy(13, 1)
+        quant_f(14)
+        mx2(14, 0)
+        mx2(14, 1)
+        regroup(15)
+        quant_f(15)
+        mx2(15, 0)
+        mx2(15, 1)
+        out_copy(14, 0)
+        out_copy(14, 1)
+        regroup(16)
+        quant_f(16)
+        out_copy(15, 0)
+        out_copy(15, 1)
+        mx2(16, 0)
+        mx2(16, 1)
+        out_copy(16, 0)
+        out_copy(16, 1)

@@ -27,15 +27,15 @@ TAIL_FROM = 14
 
 
 def norm_engine(s, j):
-    return "s"
+    return "t" if s >= 1 and j < 2 else "s"
 
 
 def copy_engine_out(s, h):
-    return "s" if (h == 1 or s >= 12) else "v"
+    return "s" if (h == 1 or s % 2 == 0) else "v"
 
 
 def copy_engine_x(s, b):
-    return "v"
+    return "v" if b % 2 == 0 else "s"
 
 
 def copy_engine_nb(s):
@@ -132,7 +132,6 @@ def tile_nnk_t_kernel(tc, x, input_weights, xis, proj_matrix, out):
         )
         nc.vector.tensor_scalar_add(out=bias[:], in0=xs[:], scalar1=-HALF_LN_R)
 
-        junks = const.tile([P, D], BF16, name="junks")
 
         xb_ps = ps_n.tile([P, 4, P], F32, tag="nbp", name="xb_ps")
         for t in range(4):
@@ -180,13 +179,44 @@ def tile_nnk_t_kernel(tc, x, input_weights, xis, proj_matrix, out):
         def norm(s, j):
             if not valid(s) or j >= ntiles(s):
                 return
-            eng = norm_engine(s, j)
+            if norm_engine(s, j) != "s":
+                return
+            norm_tile(s, "s")
+            xn = st[("xn", s)]
+            junk = work.tile([P, D], BF16, tag="junks", name="junks")
+            nc.scalar.activation(
+                out=junk[:], in_=xn[:, j, :], func=ACT.Square, accum_out=norm_col(s, j)
+            )
+
+        def norm_tile(s, eng):
             if ("n" + eng, s) not in st:
                 ncols = small.tile([P, 4], F32, tag="n" + eng, name="ncols")
                 st[("n" + eng, s)] = ncols
-            xn = st[("xn", s)]
-            nc.scalar.activation(
-                out=junks[:], in_=xn[:, j, :], func=ACT.Square, accum_out=norm_col(s, j)
+
+        def gram(s):
+            if not valid(s) or s == 0:
+                return
+            xg = st[("xg", s)]
+            gp = ps_n.tile([P, 2, P], F32, tag="nbp", name="gp")
+            for j in range(2):
+                for k in range(8):
+                    xk = xg[:, k // 4, j * P : (j + 1) * P, k % 4]
+                    nc.tensor.matmul(gp[:, j, :], lhsT=xk, rhs=xk, start=(k == 0), stop=(k == 7))
+            st[("gp", s)] = gp
+
+        def diag(s, j):
+            if not valid(s) or s == 0:
+                return
+            norm_tile(s, "t")
+            junk = work.tile([P, P], F32, tag="junkv", name="junkv")
+            nc.vector.scalar_tensor_tensor(
+                out=junk[:],
+                in0=st[("gp", s)][:, j, :],
+                scalar=1.0,
+                in1=ident[:],
+                op0=ALU.mult,
+                op1=ALU.mult,
+                accum_out=norm_col(s, j),
             )
 
         def banks(s):
@@ -210,7 +240,7 @@ def tile_nnk_t_kernel(tc, x, input_weights, xis, proj_matrix, out):
         def xo(s, b):
             if not valid(s) or b >= len(banks(s)):
                 return
-            if b == 0:
+            if ("xg", s) not in st:
                 xg = work.tile([P, 2, ntiles(s) * P, 4], BF16, tag="xg", name="xg", align_bytes=64)
                 st[("xg", s)] = xg
             xg32 = st[("xg", s)][:].bitcast(F32)
@@ -391,96 +421,101 @@ def tile_nnk_t_kernel(tc, x, input_weights, xis, proj_matrix, out):
         g_multiply(1, 0)
         g_multiply(1, 1)
         load(4)
-        for j in range(4):
-            norm(1, j)
+        norm(1, 2)
+        norm(1, 3)
         xt(1, [0, 1])
         xo(1, 0)
         xo(1, 1)
+        nb_pe(0)
+        nb_copy(0)
         quant_g()
         quant_x(0)
         xt(1, [2, 3])
         load(5)
         xo(1, 2)
         xo(1, 3)
-        nb_pe(0)
-        nb_copy(0)
+        gram(1)
+        diag(1, 0)
+        diag(1, 1)
         quant_x(1)
-        for j in range(4):
-            norm(2, j)
-        xt(2, [0, 1])
+        norm(2, 2)
+        norm(2, 3)
         for t in range(4):
             mx1(0, t)
+        xt(2, [0, 1])
         nb_pe(1)
         load(6)
         xo(2, 0)
         xo(2, 1)
         for t in range(4):
             stt(0, t)
+        nb_copy(1)
         expo(0, 0)
-        norm(3, 0)
-        norm(3, 1)
         expo(0, 1)
         expo(0, 2)
         expo(0, 3)
-        norm(3, 2)
         xt(2, [2, 3])
         xo(2, 2)
         xo(2, 3)
         for t in range(4):
             mx1(1, t)
-        nb_copy(1)
+        norm(3, 2)
+        norm(3, 3)
         quant_x(2)
         xt(3, [0, 1])
-        nb_pe(2)
         load(7)
 
         for i in range(1, NG - 2):
-            quant_f(i - 2)
-            out_copy(i - 3, 1)
-            stt(i, 0)
-            norm(i + 2, 3)
-            xo(i + 2, 0)
             regroup(i - 1)
+            gram(i + 1)
+            stt(i, 0)
             xo(i + 2, 1)
+            out_copy(i - 3, 1)
+            xo(i + 2, 0)
             load(i + 7)
             expo(i, 0)
             stt(i, 1)
-            xt(i + 2, [2, 3])
-            norm(i + 3, 0)
-            stt(i, 2)
             mx1(i + 1, 0)
-            stt(i, 3)
-            mx2(i - 2, 0)
-            norm(i + 3, 1)
-            xo(i + 2, 2)
-            mx1(i + 1, 1)
-            xo(i + 2, 3)
-            mx1(i + 1, 2)
-            expo(i, 1)
-            nb_copy(i + 1)
-            mx1(i + 1, 3)
-            expo(i, 2)
-            expo(i, 3)
-            out_copy(i - 2, 0)
-            xt(i + 3, [0, 1])
-            quant_x(i + 2)
-            nb_pe(i + 2)
             norm(i + 3, 2)
+            diag(i + 1, 0)
+            diag(i + 1, 1)
+            xt(i + 2, [2, 3])
+            nb_pe(i + 1)
+            stt(i, 2)
+            expo(i, 1)
+            xo(i + 2, 2)
+            xo(i + 2, 3)
+            mx1(i + 1, 1)
+            mx2(i - 2, 0)
+            nb_copy(i + 1)
+            stt(i, 3)
+            expo(i, 2)
+            xt(i + 3, [0, 1])
+            out_copy(i - 2, 0)
+            mx1(i + 1, 2)
+            mx1(i + 1, 3)
+            norm(i + 3, 3)
+            expo(i, 3)
+            quant_x(i + 2)
             mx2(i - 2, 1)
+            quant_f(i - 1)
 
-        quant_f(13)
-        out_copy(12, 1)
+        gram(16)
         regroup(14)
+        out_copy(12, 1)
+        mx2(13, 0)
+        diag(16, 0)
+        diag(16, 1)
+        nb_pe(16)
         for t in range(4):
             stt(15, t)
         for t in range(4):
             expo(15, t)
+        nb_copy(16)
         mx1(16, 0)
-        mx2(13, 0)
         mx1(16, 1)
         mx1(16, 2)
         mx1(16, 3)
-        nb_copy(16)
         out_copy(13, 0)
         mx2(13, 1)
         for t in range(4):

@@ -24,22 +24,27 @@ HALF_LN_R = 4.5 * 0.6931471805599453
 MANUAL = True
 XBUFS = 6
 TAIL_FROM = 14
+GT = (1, 2)
+
+
+def gram_tiles(s):
+    return 0 if s < 2 else 1 if s < 4 else GT[s % 2]
 
 
 def norm_engine(s, j):
-    return "t" if s >= 1 and j < 2 else "s"
+    return "t" if j < gram_tiles(s) else "s"
 
 
 def copy_engine_out(s, h):
-    return "s" if (h == 1 or s % 2 == 0) else "v"
+    return "s" if (h == 0 or s % 2 == 0 or s > 10) else "v"
 
 
 def copy_engine_x(s, b):
-    return "v" if b % 2 == 0 else "s"
+    return "v" if b != 3 or s == 0 else "s"
 
 
 def copy_engine_nb(s):
-    return "v"
+    return "s" if s == 1 else "v"
 
 
 def regroup_engine(s):
@@ -60,6 +65,7 @@ def tile_nnk_t_kernel(tc, x, input_weights, xis, proj_matrix, out):
         ps_d = ctx.enter_context(tc.psum_pool(name="ps_d", bufs=4))
         ps_o = ctx.enter_context(tc.psum_pool(name="ps_o", bufs=1))
         ps_n = ctx.enter_context(tc.psum_pool(name="ps_n", bufs=1))
+        nbpool = ctx.enter_context(tc.tile_pool(name="nbpool", bufs=3))
         single = ctx.enter_context(tc.tile_pool(name="single", bufs=1))
         if MANUAL:
             ctx.enter_context(tc.manual_schedule())
@@ -106,15 +112,18 @@ def tile_nnk_t_kernel(tc, x, input_weights, xis, proj_matrix, out):
         pj = const.tile([P, 4, D], BF16, name="pj")
         xn_w = xpool.tile([P, 2, D], BF16, tag="xn", name="xn_w")
         st[("xn", 0)] = xn_w
-        load_proj_rows(0)
-        load_proj_rows(1)
         load_w_tile(0)
-        load_proj_rows(2)
-        load_proj_rows(3)
         load_w_tile(1)
+        for t in range(4):
+            load_proj_rows(t)
         for s in range(1, 4):
             load(s)
 
+        ncs = []
+        for b in range(4):
+            nct = const.tile([P, P], F32, name="nct%d" % b)
+            nc.gpsimd.memset(nct[:], 0.0)
+            ncs.append(nct)
         ident = const.tile([P, P], F32, name="ident")
         make_identity(nc, ident[:])
 
@@ -133,35 +142,30 @@ def tile_nnk_t_kernel(tc, x, input_weights, xis, proj_matrix, out):
         nc.vector.tensor_scalar_add(out=bias[:], in0=xs[:], scalar1=-HALF_LN_R)
 
 
-        xb_ps = ps_n.tile([P, 4, P], F32, tag="nbp", name="xb_ps")
-        for t in range(4):
-            nc.tensor.transpose(xb_ps[:, t, :], xs[:, t : t + 1].to_broadcast([P, P]), ident[:])
-        xisb = const.tile([P, 4, P], F32, name="xisb")
-        nc.vector.tensor_copy(out=xisb[:], in_=xb_ps[:])
-
         gg = const.tile([P, 2, R, 4], BF16, name="gg", align_bytes=64)
         gc = const.tile([P, 2, R], U32, name="gc", align_bytes=64)
         gsc = const.tile([P, 2, R], U8, name="gsc", align_bytes=64)
-        pjw = pj[:].bitcast(F32)
+        gr = const.tile([P, 4, D], BF16, name="gr")
+        grw = gr[:].bitcast(F32)
+        gg32 = gg[:].bitcast(F32)
+
+        def g_multiply(t):
+            nc.vector.tensor_scalar_mul(out=gr[:, t, :], in0=pj[:, t, :], scalar1=xs[:, t : t + 1])
 
         def g_transposes(h, g):
             pg = ps_d.tile([P, 2, 2, P], F32, tag="d", name="pg")
-            for tt in range(2):
-                for u in range(2):
+            for u in range(2):
+                for tt in range(2):
                     w0 = 256 * g + 128 * u
-                    nc.tensor.transpose(pg[:, tt, u, :], pjw[:, 2 * h + tt, w0 : w0 + P], ident[:])
+                    nc.tensor.transpose(pg[:, u, tt, :], grw[:, 2 * h + tt, w0 : w0 + P], ident[:])
             st[("pg", h, g)] = pg
 
-        def g_multiply(h, g):
-            pg = st[("pg", h, g)]
-            for tt in range(2):
-                tp = 2 * h + tt
-                nc.vector.tensor_tensor(
-                    out=gg[:, g, tp * P : (tp + 1) * P, :].rearrange("p q (u e) -> p q u e", e=2),
-                    in0=pg[:, tt].bitcast(BF16).rearrange("p u (q e) -> p q u e", e=2),
-                    in1=xisb[:, tp, :].unsqueeze(2).unsqueeze(3).to_broadcast([P, P, 2, 2]),
-                    op=ALU.mult,
-                )
+        def g_out(h, g):
+            psum_copy(
+                "v" if h == 0 else "s",
+                gg32[:, g, h * 256 : (h + 1) * 256, :],
+                st[("pg", h, g)][:].rearrange("p u t c -> p (t c) u"),
+            )
 
         def quant_g():
             nc.vector.quantize_mx(
@@ -174,40 +178,33 @@ def tile_nnk_t_kernel(tc, x, input_weights, xis, proj_matrix, out):
         wsc = const.tile([P, O], U8, name="wsc", align_bytes=64)
 
         def norm_col(s, j):
-            return st[("n" + norm_engine(s, j), s)][:, j : j + 1]
+            return ncs[s % 4][:, j : j + 1]
 
         def norm(s, j):
             if not valid(s) or j >= ntiles(s):
                 return
             if norm_engine(s, j) != "s":
                 return
-            norm_tile(s, "s")
             xn = st[("xn", s)]
             junk = work.tile([P, D], BF16, tag="junks", name="junks")
             nc.scalar.activation(
                 out=junk[:], in_=xn[:, j, :], func=ACT.Square, accum_out=norm_col(s, j)
             )
 
-        def norm_tile(s, eng):
-            if ("n" + eng, s) not in st:
-                ncols = small.tile([P, 4], F32, tag="n" + eng, name="ncols")
-                st[("n" + eng, s)] = ncols
-
         def gram(s):
-            if not valid(s) or s == 0:
+            if not valid(s) or gram_tiles(s) == 0:
                 return
             xg = st[("xg", s)]
             gp = ps_n.tile([P, 2, P], F32, tag="nbp", name="gp")
-            for j in range(2):
+            for j in range(gram_tiles(s)):
                 for k in range(8):
                     xk = xg[:, k // 4, j * P : (j + 1) * P, k % 4]
                     nc.tensor.matmul(gp[:, j, :], lhsT=xk, rhs=xk, start=(k == 0), stop=(k == 7))
             st[("gp", s)] = gp
 
         def diag(s, j):
-            if not valid(s) or s == 0:
+            if not valid(s) or j >= gram_tiles(s):
                 return
-            norm_tile(s, "t")
             junk = work.tile([P, P], F32, tag="junkv", name="junkv")
             nc.vector.scalar_tensor_tensor(
                 out=junk[:],
@@ -274,6 +271,30 @@ def tile_nnk_t_kernel(tc, x, input_weights, xis, proj_matrix, out):
                 nc.tensor.transpose(nbp[:, j, :], norm_col(s, j).to_broadcast([P, P]), ident[:])
             st[("nbp", s)] = nbp
 
+        def parked(s):
+            return of[(NX - 1) * GROUP + 2 * s : (NX - 1) * GROUP + 2 * s + 2, :]
+
+        def nrow_pe(s):
+            if not valid(s):
+                return
+            nrp = ps_n.tile([P, P], F32, tag="nbp", name="nrp")
+            nc.tensor.transpose(nrp[:], ncs[s % 4][:], ident[:])
+            st[("nrp", s)] = nrp
+
+        def nrow_copy(s):
+            if not valid(s):
+                return
+            nr = small.tile([P, P], F32, tag="nr", name="nr")
+            nc.vector.tensor_copy(out=nr[:], in_=st[("nrp", s)][:])
+            nc.sync.dma_start(out=parked(s).rearrange("a (b c) -> (a b) c", c=P), in_=nr[:4, :])
+
+        def nb_load(s):
+            if not valid(s):
+                return
+            nb = nbpool.tile([P, 4 * P], F32, tag="nbl", name="nb")
+            nc.sync.dma_start(out=nb[:], in_=parked(s).rearrange("a b -> (a b)").partition_broadcast(P))
+            st[("nb", s)] = nb
+
         def nb_copy(s):
             if not valid(s):
                 return
@@ -286,87 +307,101 @@ def tile_nnk_t_kernel(tc, x, input_weights, xis, proj_matrix, out):
             if not valid(s):
                 return
             n = ntiles(s) * P
-            xc = st[("xc", s)]
-            xsc = st[("xsc", s)]
             d = ps_d.tile([P, n], F32, tag="d", name="d")
             for g in range(2):
                 nc.tensor.matmul_mx(
                     out=d[:],
                     lhsT=gc[:, g, t * P : (t + 1) * P].bitcast(FP8X4),
                     lhsT_scale=gsc[:, g, t * P : (t + 1) * P],
-                    rhs=xc[:, g, :].bitcast(FP8X4),
-                    rhs_scale=xsc[:, g, :],
+                    rhs=st[("xc", s)][:, g, :].bitcast(FP8X4),
+                    rhs_scale=st[("xsc", s)][:, g, :],
                     start=(g == 0),
                     stop=(g == 1),
                 )
             st[("d", s, t)] = d
 
-        def stt(s, t):
+        def cols(s, half):
+            n = ntiles(s) * P
+            return slice(0, n) if half is None else slice(half * n // 2, (half + 1) * n // 2)
+
+        def stt(s, t, half=None):
             if not valid(s):
                 return
             n = ntiles(s) * P
-            if t == 0:
+            c = cols(s, half)
+            if ("z", s) not in st:
                 z = work.tile([P, 4, n], F32, tag="z", name="z")
                 st[("z", s)] = z
             nc.vector.scalar_tensor_tensor(
-                out=st[("z", s)][:, t, :],
-                in0=st[("nb", s)][:],
+                out=st[("z", s)][:, t, c],
+                in0=st[("nb", s)][:, c],
                 scalar=nega[:, t : t + 1],
-                in1=st[("d", s, t)][:],
+                in1=st[("d", s, t)][:, c],
                 op0=ALU.mult,
                 op1=ALU.add,
             )
 
-        def expo(s, t):
+        def expo(s, t, half=None):
             if not valid(s):
                 return
             n = ntiles(s) * P
-            if t == 0:
+            c = cols(s, half)
+            if ("f", s) not in st:
                 f = work.tile([P, 4, n], BF16, tag="f", name="f")
                 st[("f", s)] = f
             nc.scalar.activation(
-                out=st[("f", s)][:, t, :],
-                in_=st[("z", s)][:, t, :],
+                out=st[("f", s)][:, t, c],
+                in_=st[("z", s)][:, t, c],
                 func=ACT.Exp,
                 bias=bias[:, t : t + 1],
                 scale=1.0,
             )
 
-        def regroup(s):
+        def regroup(s, half=None):
             if not valid(s):
                 return
             n = ntiles(s) * P
-            fg = single.tile([P, n, 4], BF16, tag="fg", name="fg", align_bytes=64)
+            c = cols(s, half)
+            if ("fg", s) not in st:
+                if s >= NG - 2:
+                    fg = work.tile([P, n, 4], BF16, tag="fgt", name="fg", align_bytes=64)
+                else:
+                    fg = single.tile([P, n, 4], BF16, tag="fg", name="fg", align_bytes=64)
+                st[("fg", s)] = fg
+            fg = st[("fg", s)]
             if regroup_engine(s) == "v":
                 nc.vector.tensor_copy(
-                    out=fg[:].rearrange("p (c i) t -> p c t i", i=4),
-                    in_=st[("f", s)][:].rearrange("p t (c i) -> p c t i", i=4),
+                    out=fg[:, c, :].rearrange("p (c i) t -> p c t i", i=4),
+                    in_=st[("f", s)][:, :, c].rearrange("p t (c i) -> p c t i", i=4),
                 )
             else:
                 nc.gpsimd.tensor_scalar(
-                    out=fg[:],
-                    in0=st[("f", s)][:].rearrange("p t n -> p n t"),
+                    out=fg[:, c, :],
+                    in0=st[("f", s)][:, :, c].rearrange("p t n -> p n t"),
                     scalar1=1.0,
                     scalar2=0.0,
                     op0=ALU.mult,
                     op1=ALU.add,
                 )
-            st[("fg", s)] = fg
 
-        def quant_f(s):
+        def quant_f(s, half=None):
             if not valid(s):
                 return
             n = ntiles(s) * P
+            c = cols(s, half)
             if s == 0:
                 fc = wc
                 fsc = wsc
+            elif ("fc", s) in st:
+                fc = st[("fc", s)]
+                fsc = st[("fsc", s)]
             else:
                 fc = work.tile([P, n], U32, tag="fc", name="fc", align_bytes=64)
                 fsc = work.tile([P, n], U8, tag="fsc", name="fsc", align_bytes=64)
             nc.vector.quantize_mx(
-                out=fc[:].bitcast(FP8X4),
-                scales=fsc[:],
-                in_=st[("fg", s)][:].rearrange("p n t -> p (n t)"),
+                out=fc[:, c].bitcast(FP8X4),
+                scales=fsc[:, c],
+                in_=st[("fg", s)][:, c, :].rearrange("p n t -> p (n t)"),
             )
             st[("fc", s)] = fc
             st[("fsc", s)] = fsc
@@ -374,8 +409,6 @@ def tile_nnk_t_kernel(tc, x, input_weights, xis, proj_matrix, out):
         def mx2(s, h):
             if not (1 <= s < NG):
                 return
-            fc = st[("fc", s)]
-            fsc = st[("fsc", s)]
             if s >= TAIL_FROM:
                 o = ps_d.tile([P, 2, O], F32, tag="d", name="o")
             else:
@@ -384,8 +417,8 @@ def tile_nnk_t_kernel(tc, x, input_weights, xis, proj_matrix, out):
                 j = 2 * h + jj
                 nc.tensor.matmul_mx(
                     out=o[:, jj, :],
-                    lhsT=fc[:, j * P : (j + 1) * P].bitcast(FP8X4),
-                    lhsT_scale=fsc[:, j * P : (j + 1) * P],
+                    lhsT=st[("fc", s)][:, j * P : (j + 1) * P].bitcast(FP8X4),
+                    lhsT_scale=st[("fsc", s)][:, j * P : (j + 1) * P],
                     rhs=wc[:].bitcast(FP8X4),
                     rhs_scale=wsc[:],
                     start=True,
@@ -407,136 +440,159 @@ def tile_nnk_t_kernel(tc, x, input_weights, xis, proj_matrix, out):
             elif h == 1:
                 nc.sync.dma_start(out=dst, in_=osb[:])
 
-        g_transposes(0, 0)
-        g_transposes(0, 1)
-        g_multiply(0, 0)
-        g_multiply(0, 1)
+        xt(0, [0, 1])
         norm(0, 0)
         norm(0, 1)
-        xt(0, [0, 1])
         xo(0, 0)
+        g_multiply(0)
+        g_multiply(1)
+        g_transposes(0, 0)
+        g_transposes(0, 1)
         xo(0, 1)
+        g_multiply(2)
+        g_multiply(3)
         g_transposes(1, 0)
         g_transposes(1, 1)
-        g_multiply(1, 0)
-        g_multiply(1, 1)
+        g_out(0, 0)
+        g_out(0, 1)
+        nb_pe(0)
+        quant_x(0)
+        g_out(1, 0)
+        g_out(1, 1)
         load(4)
-        norm(1, 2)
-        norm(1, 3)
         xt(1, [0, 1])
         xo(1, 0)
         xo(1, 1)
-        nb_pe(0)
-        nb_copy(0)
-        quant_g()
-        quant_x(0)
         xt(1, [2, 3])
+        quant_g()
+        norm(1, 0)
+        norm(1, 1)
+        nb_copy(0)
         load(5)
         xo(1, 2)
         xo(1, 3)
-        gram(1)
-        diag(1, 0)
-        diag(1, 1)
-        quant_x(1)
+        norm(1, 2)
+        norm(1, 3)
         norm(2, 2)
-        norm(2, 3)
-        for t in range(4):
-            mx1(0, t)
         xt(2, [0, 1])
+        for t in range(3):
+            mx1(0, t)
+        quant_x(1)
         nb_pe(1)
-        load(6)
+        nb_copy(1)
+        norm(2, 3)
+        norm(2, 1)
         xo(2, 0)
         xo(2, 1)
-        for t in range(4):
-            stt(0, t)
-        nb_copy(1)
-        expo(0, 0)
-        expo(0, 1)
-        expo(0, 2)
-        expo(0, 3)
         xt(2, [2, 3])
-        xo(2, 2)
-        xo(2, 3)
-        for t in range(4):
-            mx1(1, t)
-        norm(3, 2)
-        norm(3, 3)
-        quant_x(2)
-        xt(3, [0, 1])
-        load(7)
+        load(6)
 
-        for i in range(1, NG - 2):
-            regroup(i - 1)
-            gram(i + 1)
+        for i in range(0, NG - 3):
+            gram(i + 2)
             stt(i, 0)
-            xo(i + 2, 1)
-            out_copy(i - 3, 1)
-            xo(i + 2, 0)
-            load(i + 7)
-            expo(i, 0)
-            stt(i, 1)
-            mx1(i + 1, 0)
-            norm(i + 3, 2)
-            diag(i + 1, 0)
-            diag(i + 1, 1)
-            xt(i + 2, [2, 3])
-            nb_pe(i + 1)
-            stt(i, 2)
-            expo(i, 1)
-            xo(i + 2, 2)
+            expo(i - 1, 3)
             xo(i + 2, 3)
-            mx1(i + 1, 1)
-            mx2(i - 2, 0)
-            nb_copy(i + 1)
-            stt(i, 3)
-            expo(i, 2)
-            xt(i + 3, [0, 1])
-            out_copy(i - 2, 0)
-            mx1(i + 1, 2)
-            mx1(i + 1, 3)
-            norm(i + 3, 3)
-            expo(i, 3)
+            stt(i, 1)
+            mx1(i, 3)
+            xo(i + 2, 2)
+            expo(i, 0)
+            norm(i + 3, 2)
+            mx1(i + 1, 0)
+            mx2(i - 3, 1)
+            stt(i, 2)
+            diag(i + 2, 0)
+            diag(i + 2, 1)
             quant_x(i + 2)
-            mx2(i - 2, 1)
-            quant_f(i - 1)
+            nrow_pe(i + 2)
+            xt(i + 3, [0, 1])
+            expo(i, 1)
+            quant_f(i - 2)
+            out_copy(i - 3, 1)
+            nrow_copy(i + 2)
+            regroup(i - 1)
+            load(i + 7)
+            xo(i + 3, 0)
+            norm(i + 3, 3)
+            norm(i + 3, 1)
+            xo(i + 3, 1)
+            mx1(i + 1, 1)
+            mx1(i + 1, 2)
+            mx2(i - 2, 0)
+            stt(i, 3)
+            nb_load(i + 2)
+            expo(i, 2)
+            out_copy(i - 2, 0)
+            xt(i + 3, [2, 3])
 
         gram(16)
-        regroup(14)
-        out_copy(12, 1)
-        mx2(13, 0)
+        stt(14, 0)
+        xo(16, 3)
+        xo(16, 2)
+        expo(13, 3)
+        mx1(14, 3)
+        stt(14, 1)
+        expo(14, 0)
         diag(16, 0)
         diag(16, 1)
-        nb_pe(16)
-        for t in range(4):
-            stt(15, t)
-        for t in range(4):
-            expo(15, t)
-        nb_copy(16)
+        quant_x(16)
+        quant_f(12)
+        mx1(15, 0)
+        nrow_pe(16)
+        mx2(11, 1)
+        regroup(13)
+        expo(14, 1)
+        stt(14, 2)
+        mx1(15, 1)
+        nrow_copy(16)
+        stt(14, 3)
+        mx1(15, 2)
+        mx2(12, 0)
+        out_copy(11, 1)
+        expo(14, 2)
+        stt(15, 0)
+        nb_load(16)
+        mx1(15, 3)
         mx1(16, 0)
+        expo(14, 3)
+        out_copy(12, 0)
+        stt(15, 1)
+        expo(15, 0)
         mx1(16, 1)
+        mx2(12, 1)
+        stt(15, 2)
+        expo(15, 1)
+        stt(15, 3)
+        expo(15, 2)
+        quant_f(13)
+        regroup(14)
+        out_copy(12, 1)
+        expo(15, 3)
+        mx2(13, 0)
         mx1(16, 2)
         mx1(16, 3)
-        out_copy(13, 0)
-        mx2(13, 1)
         for t in range(4):
             stt(16, t)
+        out_copy(13, 0)
         for t in range(4):
             expo(16, t)
-        out_copy(13, 1)
+        mx2(13, 1)
         quant_f(14)
+        regroup(15)
         mx2(14, 0)
         mx2(14, 1)
-        regroup(15)
+        out_copy(13, 1)
         quant_f(15)
+        out_copy(14, 0)
         mx2(15, 0)
         mx2(15, 1)
-        out_copy(14, 0)
         out_copy(14, 1)
-        regroup(16)
-        quant_f(16)
+        regroup(16, 0)
         out_copy(15, 0)
         out_copy(15, 1)
+        quant_f(16, 0)
+        regroup(16, 1)
         mx2(16, 0)
-        mx2(16, 1)
+        quant_f(16, 1)
         out_copy(16, 0)
+        mx2(16, 1)
         out_copy(16, 1)

@@ -36,7 +36,7 @@ def norm_engine(s, j):
 
 
 def copy_engine_out(s, h):
-    return "s" if (h == 0 or s % 2 == 0 or s > 10) else "v"
+    return "s" if (h == 0 or s % 2 == 1 or s > 10) else "v"
 
 
 def copy_engine_x(s, b):
@@ -44,7 +44,7 @@ def copy_engine_x(s, b):
 
 
 def copy_engine_nb(s):
-    return "s" if s == 1 else "v"
+    return "s" if s == 1 or s % 2 == 0 else "v"
 
 
 def regroup_engine(s):
@@ -65,6 +65,7 @@ def tile_nnk_t_kernel(tc, x, input_weights, xis, proj_matrix, out):
         ps_d = ctx.enter_context(tc.psum_pool(name="ps_d", bufs=4))
         ps_o = ctx.enter_context(tc.psum_pool(name="ps_o", bufs=1))
         ps_n = ctx.enter_context(tc.psum_pool(name="ps_n", bufs=1))
+        xq = ctx.enter_context(tc.tile_pool(name="xq", bufs=3))
         nbpool = ctx.enter_context(tc.tile_pool(name="nbpool", bufs=3))
         single = ctx.enter_context(tc.tile_pool(name="single", bufs=1))
         if MANUAL:
@@ -252,8 +253,8 @@ def tile_nnk_t_kernel(tc, x, input_weights, xis, proj_matrix, out):
             if not valid(s):
                 return
             n = ntiles(s) * P
-            xc = work.tile([P, 2, n], U32, tag="xc", name="xc", align_bytes=64)
-            xsc = work.tile([P, 2, n], U8, tag="xsc", name="xsc", align_bytes=64)
+            xc = xq.tile([P, 2, n], U32, tag="xc", name="xc", align_bytes=64)
+            xsc = xq.tile([P, 2, n], U8, tag="xsc", name="xsc", align_bytes=64)
             nc.vector.quantize_mx(
                 out=xc[:].rearrange("p g n -> p (g n)").bitcast(FP8X4),
                 scales=xsc[:].rearrange("p g n -> p (g n)"),
@@ -299,7 +300,7 @@ def tile_nnk_t_kernel(tc, x, input_weights, xis, proj_matrix, out):
             if not valid(s):
                 return
             nt = ntiles(s)
-            nb = work.tile([P, nt * P], F32, tag="nb", name="nb")
+            nb = nbpool.tile([P, nt * P], F32, tag="nb", name="nb")
             psum_copy(copy_engine_nb(s), nb[:], st[("nbp", s)][:].rearrange("p j c -> p (j c)"))
             st[("nb", s)] = nb
 
@@ -503,12 +504,12 @@ def tile_nnk_t_kernel(tc, x, input_weights, xis, proj_matrix, out):
             diag(i + 2, 0)
             diag(i + 2, 1)
             quant_x(i + 2)
-            nrow_pe(i + 2)
+            nb_pe(i + 2)
             xt(i + 3, [0, 1])
             expo(i, 1)
             quant_f(i - 2)
             out_copy(i - 3, 1)
-            nrow_copy(i + 2)
+            nb_copy(i + 2)
             regroup(i - 1)
             load(i + 7)
             xo(i + 3, 0)
@@ -519,7 +520,6 @@ def tile_nnk_t_kernel(tc, x, input_weights, xis, proj_matrix, out):
             mx1(i + 1, 2)
             mx2(i - 2, 0)
             stt(i, 3)
-            nb_load(i + 2)
             expo(i, 2)
             out_copy(i - 2, 0)
             xt(i + 3, [2, 3])
@@ -537,20 +537,19 @@ def tile_nnk_t_kernel(tc, x, input_weights, xis, proj_matrix, out):
         quant_x(16)
         quant_f(12)
         mx1(15, 0)
-        nrow_pe(16)
+        nb_pe(16)
         mx2(11, 1)
         regroup(13)
         expo(14, 1)
         stt(14, 2)
         mx1(15, 1)
-        nrow_copy(16)
+        nb_copy(16)
         stt(14, 3)
         mx1(15, 2)
         mx2(12, 0)
         out_copy(11, 1)
         expo(14, 2)
         stt(15, 0)
-        nb_load(16)
         mx1(15, 3)
         mx1(16, 0)
         expo(14, 3)

@@ -36,15 +36,15 @@ def norm_engine(s, j):
 
 
 def copy_engine_out(s, h):
-    return "s" if (h == 0 or s % 2 == 1 or s > 10) else "v"
+    return "s"
 
 
 def copy_engine_x(s, b):
-    return "v" if b != 3 or s == 0 else "s"
+    return "v"
 
 
 def copy_engine_nb(s):
-    return "s" if s == 1 or s % 2 == 0 else "v"
+    return "s"
 
 
 def regroup_engine(s):

@@ -58,7 +58,7 @@ def tile_nnk_t_kernel(tc, x, input_weights, xis, proj_matrix, out):
     with ExitStack() as ctx:
         const = ctx.enter_context(tc.tile_pool(name="const", bufs=1))
         xpool = ctx.enter_context(tc.tile_pool(name="xpool", bufs=XBUFS))
-        work = ctx.enter_context(tc.tile_pool(name="work", bufs=2))
+        work = ctx.enter_context(tc.tile_pool(name="work", bufs=3))
         small = ctx.enter_context(tc.tile_pool(name="small", bufs=4))
         opool = ctx.enter_context(tc.tile_pool(name="opool", bufs=4))
         ps_xt = ctx.enter_context(tc.psum_pool(name="ps_xt", bufs=2))
@@ -103,6 +103,15 @@ def tile_nnk_t_kernel(tc, x, input_weights, xis, proj_matrix, out):
                 in_=input_weights.rearrange("(j p) k -> p j k", p=P)[:, j, :],
             )
 
+        def load_first(h):
+            if h == 0:
+                xn = xpool.tile([P, 4, D], BF16, tag="xn", name="xn")
+                st[("xn", 1)] = xn
+            src = xf[:GROUP, :].rearrange("(p j) k -> p j k", j=4)
+            nc.sync.dma_start(
+                out=st[("xn", 1)][:, 2 * h : 2 * h + 2, :], in_=src[:, 2 * h : 2 * h + 2, :]
+            )
+
         def load_proj_rows(t):
             nc.sync.dma_start(
                 out=pj[:, t, :], in_=proj_matrix.rearrange("(p t) k -> p t k", t=4)[:, t, :]
@@ -115,10 +124,12 @@ def tile_nnk_t_kernel(tc, x, input_weights, xis, proj_matrix, out):
         st[("xn", 0)] = xn_w
         load_w_tile(0)
         load_w_tile(1)
+        load_first(0)
         for t in range(4):
             load_proj_rows(t)
-        for s in range(1, 4):
-            load(s)
+        load_first(1)
+        load(2)
+        load(3)
 
         ncs = []
         for b in range(4):
@@ -163,7 +174,7 @@ def tile_nnk_t_kernel(tc, x, input_weights, xis, proj_matrix, out):
 
         def g_out(h, g):
             psum_copy(
-                "v" if h == 0 else "s",
+                "v" if (h, g) == (0, 0) else "s",
                 gg32[:, g, h * 256 : (h + 1) * 256, :],
                 st[("pg", h, g)][:].rearrange("p u t c -> p (t c) u"),
             )
@@ -445,46 +456,46 @@ def tile_nnk_t_kernel(tc, x, input_weights, xis, proj_matrix, out):
         norm(0, 0)
         norm(0, 1)
         xo(0, 0)
-        g_multiply(0)
-        g_multiply(1)
-        g_transposes(0, 0)
-        g_transposes(0, 1)
         xo(0, 1)
-        g_multiply(2)
-        g_multiply(3)
-        g_transposes(1, 0)
-        g_transposes(1, 1)
-        g_out(0, 0)
-        g_out(0, 1)
-        nb_pe(0)
-        quant_x(0)
-        g_out(1, 0)
-        g_out(1, 1)
-        load(4)
         xt(1, [0, 1])
-        xo(1, 0)
-        xo(1, 1)
-        xt(1, [2, 3])
-        quant_g()
+        g_multiply(0)
+        quant_x(0)
+        g_multiply(1)
         norm(1, 0)
         norm(1, 1)
-        nb_copy(0)
-        load(5)
+        xo(1, 0)
+        g_multiply(2)
+        g_multiply(3)
+        xo(1, 1)
+        g_transposes(0, 0)
+        g_transposes(0, 1)
+        nb_pe(0)
+        g_out(0, 0)
+        g_out(0, 1)
+        g_transposes(1, 0)
+        g_transposes(1, 1)
+        xt(1, [2, 3])
+        load(4)
         xo(1, 2)
         xo(1, 3)
+        g_out(1, 0)
+        g_out(1, 1)
+        nb_copy(0)
         norm(1, 2)
         norm(1, 3)
-        norm(2, 2)
+        quant_g()
+        load(5)
         xt(2, [0, 1])
+        norm(2, 2)
         for t in range(3):
             mx1(0, t)
         quant_x(1)
+        xo(2, 0)
+        xo(2, 1)
         nb_pe(1)
         nb_copy(1)
         norm(2, 3)
         norm(2, 1)
-        xo(2, 0)
-        xo(2, 1)
         xt(2, [2, 3])
         load(6)
 
@@ -492,20 +503,20 @@ def tile_nnk_t_kernel(tc, x, input_weights, xis, proj_matrix, out):
             gram(i + 2)
             stt(i, 0)
             expo(i - 1, 3)
-            xo(i + 2, 3)
             stt(i, 1)
             mx1(i, 3)
             xo(i + 2, 2)
+            xo(i + 2, 3)
             expo(i, 0)
             norm(i + 3, 2)
             mx1(i + 1, 0)
             mx2(i - 3, 1)
             stt(i, 2)
+            quant_x(i + 2)
             diag(i + 2, 0)
             diag(i + 2, 1)
-            quant_x(i + 2)
-            nb_pe(i + 2)
             xt(i + 3, [0, 1])
+            nb_pe(i + 2)
             expo(i, 1)
             quant_f(i - 2)
             out_copy(i - 3, 1)
@@ -526,72 +537,72 @@ def tile_nnk_t_kernel(tc, x, input_weights, xis, proj_matrix, out):
 
         gram(16)
         stt(14, 0)
-        xo(16, 3)
-        xo(16, 2)
         expo(13, 3)
-        mx1(14, 3)
         stt(14, 1)
         expo(14, 0)
+        mx1(14, 3)
+        xo(16, 3)
+        xo(16, 2)
+        expo(14, 1)
+        mx1(15, 0)
         diag(16, 0)
         diag(16, 1)
-        quant_x(16)
         quant_f(12)
-        mx1(15, 0)
+        quant_x(16)
+        regroup(13)
         nb_pe(16)
         mx2(11, 1)
-        regroup(13)
-        expo(14, 1)
         stt(14, 2)
-        mx1(15, 1)
-        nb_copy(16)
-        stt(14, 3)
-        mx1(15, 2)
-        mx2(12, 0)
-        out_copy(11, 1)
         expo(14, 2)
+        nb_copy(16)
+        mx1(15, 1)
+        stt(14, 3)
+        out_copy(11, 1)
+        mx1(15, 2)
+        expo(14, 3)
         stt(15, 0)
         mx1(15, 3)
-        mx1(16, 0)
-        expo(14, 3)
-        out_copy(12, 0)
         stt(15, 1)
-        expo(15, 0)
-        mx1(16, 1)
-        mx2(12, 1)
+        mx2(12, 0)
+        mx1(16, 0)
         stt(15, 2)
+        expo(15, 0)
+        out_copy(12, 0)
         expo(15, 1)
         stt(15, 3)
-        expo(15, 2)
+        mx1(16, 1)
+        mx1(16, 2)
         quant_f(13)
         regroup(14)
-        out_copy(12, 1)
+        expo(15, 2)
         expo(15, 3)
-        mx2(13, 0)
-        mx1(16, 2)
         mx1(16, 3)
+        mx2(12, 1)
         for t in range(4):
             stt(16, t)
+        out_copy(12, 1)
+        mx2(13, 0)
+        regroup(15)
+        expo(16, 0)
+        expo(16, 1)
         out_copy(13, 0)
-        for t in range(4):
-            expo(16, t)
+        expo(16, 2)
+        expo(16, 3)
         mx2(13, 1)
         quant_f(14)
-        regroup(15)
+        quant_f(15)
         mx2(14, 0)
         mx2(14, 1)
         out_copy(13, 1)
-        quant_f(15)
-        out_copy(14, 0)
         mx2(15, 0)
         mx2(15, 1)
+        regroup(16)
+        out_copy(14, 0)
         out_copy(14, 1)
-        regroup(16, 0)
         out_copy(15, 0)
         out_copy(15, 1)
-        quant_f(16, 0)
-        regroup(16, 1)
+        quant_f(16)
         mx2(16, 0)
-        quant_f(16, 1)
-        out_copy(16, 0)
         mx2(16, 1)
+        out_copy(16, 0)
         out_copy(16, 1)

@@ -517,12 +517,13 @@ def tile_nnk_t_kernel(tc, x, input_weights, xis, proj_matrix, out):
             diag(i + 2, 1)
             xt(i + 3, [0, 1])
             nb_pe(i + 2)
+            out_copy(i - 3, 1)
             expo(i, 1)
             quant_f(i - 2)
-            out_copy(i - 3, 1)
             nb_copy(i + 2)
             regroup(i - 1)
             load(i + 7)
+            stt(i, 3)
             xo(i + 3, 0)
             norm(i + 3, 3)
             norm(i + 3, 1)
@@ -530,7 +531,6 @@ def tile_nnk_t_kernel(tc, x, input_weights, xis, proj_matrix, out):
             mx1(i + 1, 1)
             mx1(i + 1, 2)
             mx2(i - 2, 0)
-            stt(i, 3)
             expo(i, 2)
             out_copy(i - 2, 0)
             xt(i + 3, [2, 3])

@@ -23,7 +23,7 @@ FLOPS = 2 * (NTOK + O) * D * R + 2 * NTOK * R * O
 HALF_LN_R = 4.5 * 0.6931471805599453
 MANUAL = True
 XBUFS = 6
-TAIL_FROM = 14
+TAIL_FROM = 13
 GT = (1, 2)
 
 
@@ -36,7 +36,7 @@ def norm_engine(s, j):
 
 
 def copy_engine_out(s, h):
-    return "s"
+    return "v" if (s, h) in ((13, 0), (15, 1), (16, 1)) else "s"
 
 
 def copy_engine_x(s, b):
@@ -118,7 +118,7 @@ def tile_nnk_t_kernel(tc, x, input_weights, xis, proj_matrix, out):
             )
 
         xs_bf = const.tile([P, 4], BF16, name="xs_bf")
-        nc.sync.dma_start(out=xs_bf[:], in_=xis.rearrange("(p t) -> p t", t=4))
+        nc.scalar.dma_start(out=xs_bf[:], in_=xis.rearrange("(p t) -> p t", t=4))
         pj = const.tile([P, 4, D], BF16, name="pj")
         xn_w = xpool.tile([P, 2, D], BF16, tag="xn", name="xn_w")
         st[("xn", 0)] = xn_w
@@ -447,7 +447,7 @@ def tile_nnk_t_kernel(tc, x, input_weights, xis, proj_matrix, out):
             osb = st[("osb", s)]
             psum_copy(copy_engine_out(s, h), osb[:, 2 * h : 2 * h + 2, :], st[("o", s, h)][:])
             dst = of[(s - 1) * GROUP : s * GROUP, :].rearrange("(p j) o -> p j o", j=4)
-            if s == NG - 1:
+            if s >= TAIL_FROM - 1:
                 nc.sync.dma_start(out=dst[:, 2 * h : 2 * h + 2, :], in_=osb[:, 2 * h : 2 * h + 2, :])
             elif h == 1:
                 nc.sync.dma_start(out=dst, in_=osb[:])
@@ -578,30 +578,30 @@ def tile_nnk_t_kernel(tc, x, input_weights, xis, proj_matrix, out):
         expo(15, 3)
         mx1(16, 3)
         mx2(12, 1)
+        out_copy(12, 1)
         for t in range(4):
             stt(16, t)
-        out_copy(12, 1)
         mx2(13, 0)
-        regroup(15)
-        expo(16, 0)
-        expo(16, 1)
-        out_copy(13, 0)
-        expo(16, 2)
-        expo(16, 3)
         mx2(13, 1)
+        out_copy(13, 0)
+        regroup(15)
+        for t in range(4):
+            expo(16, t)
         quant_f(14)
         quant_f(15)
+        out_copy(13, 1)
         mx2(14, 0)
         mx2(14, 1)
-        out_copy(13, 1)
-        mx2(15, 0)
-        mx2(15, 1)
-        regroup(16)
+        regroup(16, 0)
+        regroup(16, 1)
         out_copy(14, 0)
         out_copy(14, 1)
+        mx2(15, 0)
+        mx2(15, 1)
         out_copy(15, 0)
+        quant_f(16, 0)
+        quant_f(16, 1)
         out_copy(15, 1)
-        quant_f(16)
         mx2(16, 0)
         mx2(16, 1)
         out_copy(16, 0)

@@ -131,11 +131,6 @@ def tile_nnk_t_kernel(tc, x, input_weights, xis, proj_matrix, out):
         load(2)
         load(3)
 
-        ncs = []
-        for b in range(4):
-            nct = const.tile([P, P], F32, name="nct%d" % b)
-            nc.gpsimd.memset(nct[:], 0.0)
-            ncs.append(nct)
         ident = const.tile([P, P], F32, name="ident")
         make_identity(nc, ident[:])
 
@@ -155,8 +150,8 @@ def tile_nnk_t_kernel(tc, x, input_weights, xis, proj_matrix, out):
 
 
         gg = const.tile([P, 2, R, 4], BF16, name="gg", align_bytes=64)
-        gc = const.tile([P, 2, R], U32, name="gc", align_bytes=64)
-        gsc = const.tile([P, 2, R], U8, name="gsc", align_bytes=64)
+        gc = const.tile([P, 2, R], U32, name="gc", align_bytes=256)
+        gsc = const.tile([P, 2, R], U8, name="gsc", align_bytes=256)
         gr = const.tile([P, 4, D], BF16, name="gr")
         grw = gr[:].bitcast(F32)
         gg32 = gg[:].bitcast(F32)
@@ -186,11 +181,14 @@ def tile_nnk_t_kernel(tc, x, input_weights, xis, proj_matrix, out):
                 in_=gg[:].rearrange("p g n t -> p (g n t)"),
             )
 
-        wc = const.tile([P, O], U32, name="wc", align_bytes=64)
-        wsc = const.tile([P, O], U8, name="wsc", align_bytes=64)
+        wc = const.tile([P, O], U32, name="wc", align_bytes=256)
+        wsc = const.tile([P, O], U8, name="wsc", align_bytes=256)
 
         def norm_col(s, j):
-            return ncs[s % 4][:, j : j + 1]
+            if ("nc", s) not in st:
+                ncol = small.tile([P, 4], F32, tag="nc", name="ncol")
+                st[("nc", s)] = ncol
+            return st[("nc", s)][:, j : j + 1]
 
         def norm(s, j):
             if not valid(s) or j >= ntiles(s):
@@ -264,8 +262,8 @@ def tile_nnk_t_kernel(tc, x, input_weights, xis, proj_matrix, out):
             if not valid(s):
                 return
             n = ntiles(s) * P
-            xc = xq.tile([P, 2, n], U32, tag="xc", name="xc", align_bytes=64)
-            xsc = xq.tile([P, 2, n], U8, tag="xsc", name="xsc", align_bytes=64)
+            xc = xq.tile([P, 2, n], U32, tag="xc", name="xc", align_bytes=256)
+            xsc = xq.tile([P, 2, n], U8, tag="xsc", name="xsc", align_bytes=256)
             nc.vector.quantize_mx(
                 out=xc[:].rearrange("p g n -> p (g n)").bitcast(FP8X4),
                 scales=xsc[:].rearrange("p g n -> p (g n)"),
@@ -282,30 +280,6 @@ def tile_nnk_t_kernel(tc, x, input_weights, xis, proj_matrix, out):
             for j in range(nt):
                 nc.tensor.transpose(nbp[:, j, :], norm_col(s, j).to_broadcast([P, P]), ident[:])
             st[("nbp", s)] = nbp
-
-        def parked(s):
-            return of[(NX - 1) * GROUP + 2 * s : (NX - 1) * GROUP + 2 * s + 2, :]
-
-        def nrow_pe(s):
-            if not valid(s):
-                return
-            nrp = ps_n.tile([P, P], F32, tag="nbp", name="nrp")
-            nc.tensor.transpose(nrp[:], ncs[s % 4][:], ident[:])
-            st[("nrp", s)] = nrp
-
-        def nrow_copy(s):
-            if not valid(s):
-                return
-            nr = small.tile([P, P], F32, tag="nr", name="nr")
-            nc.vector.tensor_copy(out=nr[:], in_=st[("nrp", s)][:])
-            nc.sync.dma_start(out=parked(s).rearrange("a (b c) -> (a b) c", c=P), in_=nr[:4, :])
-
-        def nb_load(s):
-            if not valid(s):
-                return
-            nb = nbpool.tile([P, 4 * P], F32, tag="nbl", name="nb")
-            nc.sync.dma_start(out=nb[:], in_=parked(s).rearrange("a b -> (a b)").partition_broadcast(P))
-            st[("nb", s)] = nb
 
         def nb_copy(s):
             if not valid(s):
@@ -408,8 +382,8 @@ def tile_nnk_t_kernel(tc, x, input_weights, xis, proj_matrix, out):
                 fc = st[("fc", s)]
                 fsc = st[("fsc", s)]
             else:
-                fc = work.tile([P, n], U32, tag="fc", name="fc", align_bytes=64)
-                fsc = work.tile([P, n], U8, tag="fsc", name="fsc", align_bytes=64)
+                fc = work.tile([P, n], U32, tag="fc", name="fc", align_bytes=256)
+                fsc = work.tile([P, n], U8, tag="fsc", name="fsc", align_bytes=256)
             nc.vector.quantize_mx(
                 out=fc[:, c].bitcast(FP8X4),
                 scales=fsc[:, c],

from contextlib import ExitStack

import concourse.mybir as mybir
from concourse.masks import make_identity

F32 = mybir.dt.float32
BF16 = mybir.dt.bfloat16
U32 = mybir.dt.uint32
U8 = mybir.dt.uint8
FP8X4 = mybir.dt.float8_e4m3fn_x4
ALU = mybir.AluOpType
ACT = mybir.ActivationFunctionType

P = 128
D = 1024
R = 512
O = 256
NTOK = 8192
GROUP = 512
NX = NTOK // GROUP
NG = NX + 1
FLOPS = 2 * (NTOK + O) * D * R + 2 * NTOK * R * O
HALF_LN_R = 4.5 * 0.6931471805599453
MANUAL = True
XBUFS = 6
TAIL_FROM = 13
GT = (1, 2)


def gram_tiles(s):
    return 0 if s < 2 else 1 if s < 4 else GT[s % 2]


def norm_engine(s, j):
    return "t" if j < gram_tiles(s) else "s"


def copy_engine_out(s, h):
    return "v" if (s, h) in ((13, 0), (15, 1), (16, 1)) else "s"


def copy_engine_x(s, b):
    return "v"


def copy_engine_nb(s):
    return "s"


def regroup_engine(s):
    return "v" if s >= NG - 2 else "g"


def tile_nnk_t_kernel(tc, x, input_weights, xis, proj_matrix, out):
    nc = tc.nc
    xf = x.flatten_outer_dims()
    of = out.flatten_outer_dims()
    with ExitStack() as ctx:
        const = ctx.enter_context(tc.tile_pool(name="const", bufs=1))
        xpool = ctx.enter_context(tc.tile_pool(name="xpool", bufs=XBUFS))
        work = ctx.enter_context(tc.tile_pool(name="work", bufs=3))
        small = ctx.enter_context(tc.tile_pool(name="small", bufs=4))
        opool = ctx.enter_context(tc.tile_pool(name="opool", bufs=4))
        ps_xt = ctx.enter_context(tc.psum_pool(name="ps_xt", bufs=2))
        ps_d = ctx.enter_context(tc.psum_pool(name="ps_d", bufs=4))
        ps_o = ctx.enter_context(tc.psum_pool(name="ps_o", bufs=1))
        ps_n = ctx.enter_context(tc.psum_pool(name="ps_n", bufs=1))
        xq = ctx.enter_context(tc.tile_pool(name="xq", bufs=3))
        nbpool = ctx.enter_context(tc.tile_pool(name="nbpool", bufs=3))
        single = ctx.enter_context(tc.tile_pool(name="single", bufs=1))
        if MANUAL:
            ctx.enter_context(tc.manual_schedule())

        st = {}

        def ntiles(s):
            return 2 if s == 0 else 4

        def valid(s):
            return 0 <= s < NG

        def psum_copy(eng, dst, src):
            if eng == "v":
                nc.vector.tensor_copy(out=dst, in_=src)
            else:
                nc.scalar.copy(out=dst, in_=src)

        def load(s):
            if not valid(s):
                return
            nt = ntiles(s)
            xn = xpool.tile([P, nt, D], BF16, tag="xn", name="xn")
            if s == 0:
                src = input_weights.rearrange("(j p) k -> p j k", p=P)
            else:
                src = xf[(s - 1) * GROUP : s * GROUP, :].rearrange("(p j) k -> p j k", j=4)
            nc.sync.dma_start(out=xn[:], in_=src)
            st[("xn", s)] = xn

        def load_w_tile(j):
            nc.sync.dma_start(
                out=st[("xn", 0)][:, j, :],
                in_=input_weights.rearrange("(j p) k -> p j k", p=P)[:, j, :],
            )

        def load_first(h):
            if h == 0:
                xn = xpool.tile([P, 4, D], BF16, tag="xn", name="xn")
                st[("xn", 1)] = xn
            src = xf[:GROUP, :].rearrange("(p j) k -> p j k", j=4)
            nc.sync.dma_start(
                out=st[("xn", 1)][:, 2 * h : 2 * h + 2, :], in_=src[:, 2 * h : 2 * h + 2, :]
            )

        def load_proj_rows(t):
            nc.sync.dma_start(
                out=pj[:, t, :], in_=proj_matrix.rearrange("(p t) k -> p t k", t=4)[:, t, :]
            )

        xs_bf = const.tile([P, 4], BF16, name="xs_bf")
        nc.scalar.dma_start(out=xs_bf[:], in_=xis.rearrange("(p t) -> p t", t=4))
        pj = const.tile([P, 4, D], BF16, name="pj")
        xn_w = xpool.tile([P, 2, D], BF16, tag="xn", name="xn_w")
        st[("xn", 0)] = xn_w
        load_w_tile(0)
        load_w_tile(1)
        load_first(0)
        for t in range(4):
            load_proj_rows(t)
        load_first(1)
        load(2)
        load(3)

        ident = const.tile([P, P], F32, name="ident")
        make_identity(nc, ident[:])

        warm_in = const.tile([P, 1], F32, name="warm_in")
        warm_out = const.tile([P, 1], F32, name="warm_out")
        nc.vector.memset(warm_in[:], 0.0)
        nc.scalar.activation(out=warm_out[:], in_=warm_in[:], func=ACT.Exp)

        xs = const.tile([P, 4], F32, name="xs")
        nega = const.tile([P, 4], F32, name="nega")
        bias = const.tile([P, 4], F32, name="bias")
        nc.vector.tensor_copy(out=xs[:], in_=xs_bf[:])
        nc.vector.scalar_tensor_tensor(
            out=nega[:], in0=xs[:], scalar=-0.5, in1=xs[:], op0=ALU.mult, op1=ALU.mult
        )
        nc.vector.tensor_scalar_add(out=bias[:], in0=xs[:], scalar1=-HALF_LN_R)


        gg = const.tile([P, 2, R, 4], BF16, name="gg", align_bytes=64)
        gc = const.tile([P, 2, R], U32, name="gc", align_bytes=256)
        gsc = const.tile([P, 2, R], U8, name="gsc", align_bytes=256)
        gr = const.tile([P, 4, D], BF16, name="gr")
        grw = gr[:].bitcast(F32)
        gg32 = gg[:].bitcast(F32)

        def g_multiply(t):
            nc.vector.tensor_scalar_mul(out=gr[:, t, :], in0=pj[:, t, :], scalar1=xs[:, t : t + 1])

        def g_transposes(h, g):
            pg = ps_d.tile([P, 2, 2, P], F32, tag="d", name="pg")
            for u in range(2):
                for tt in range(2):
                    w0 = 256 * g + 128 * u
                    nc.tensor.transpose(pg[:, u, tt, :], grw[:, 2 * h + tt, w0 : w0 + P], ident[:])
            st[("pg", h, g)] = pg

        def g_out(h, g):
            psum_copy(
                "v" if (h, g) == (0, 0) else "s",
                gg32[:, g, h * 256 : (h + 1) * 256, :],
                st[("pg", h, g)][:].rearrange("p u t c -> p (t c) u"),
            )

        def quant_g():
            nc.vector.quantize_mx(
                out=gc[:].rearrange("p g n -> p (g n)").bitcast(FP8X4),
                scales=gsc[:].rearrange("p g n -> p (g n)"),
                in_=gg[:].rearrange("p g n t -> p (g n t)"),
            )

        wc = const.tile([P, O], U32, name="wc", align_bytes=256)
        wsc = const.tile([P, O], U8, name="wsc", align_bytes=256)

        def norm_col(s, j):
            if ("nc", s) not in st:
                ncol = small.tile([P, 4], F32, tag="nc", name="ncol")
                st[("nc", s)] = ncol
            return st[("nc", s)][:, j : j + 1]

        def norm(s, j):
            if not valid(s) or j >= ntiles(s):
                return
            if norm_engine(s, j) != "s":
                return
            xn = st[("xn", s)]
            junk = work.tile([P, D], BF16, tag="junks", name="junks")
            nc.scalar.activation(
                out=junk[:], in_=xn[:, j, :], func=ACT.Square, accum_out=norm_col(s, j)
            )

        def gram(s):
            if not valid(s) or gram_tiles(s) == 0:
                return
            xg = st[("xg", s)]
            gp = ps_n.tile([P, 2, P], F32, tag="nbp", name="gp")
            for j in range(gram_tiles(s)):
                for k in range(8):
                    xk = xg[:, k // 4, j * P : (j + 1) * P, k % 4]
                    nc.tensor.matmul(gp[:, j, :], lhsT=xk, rhs=xk, start=(k == 0), stop=(k == 7))
            st[("gp", s)] = gp

        def diag(s, j):
            if not valid(s) or j >= gram_tiles(s):
                return
            junk = work.tile([P, P], F32, tag="junkv", name="junkv")
            nc.vector.scalar_tensor_tensor(
                out=junk[:],
                in0=st[("gp", s)][:, j, :],
                scalar=1.0,
                in1=ident[:],
                op0=ALU.mult,
                op1=ALU.mult,
                accum_out=norm_col(s, j),
            )

        def banks(s):
            return [(g, h) for h in range(ntiles(s) // 2) for g in range(2)]

        def xt(s, bs):
            if not valid(s):
                return
            xw = st[("xn", s)][:].bitcast(F32)
            for b in bs:
                if b >= len(banks(s)):
                    continue
                g, h = banks(s)[b]
                xtp = ps_xt.tile([P, 2, 2, P], F32, tag="xt", name="xtp")
                for u in range(2):
                    for jj in range(2):
                        w0 = 256 * g + 128 * u
                        nc.tensor.transpose(xtp[:, u, jj, :], xw[:, 2 * h + jj, w0 : w0 + P], ident[:])
                st[("xt", s, b)] = xtp

        def xo(s, b):
            if not valid(s) or b >= len(banks(s)):
                return
            if ("xg", s) not in st:
                xg = work.tile([P, 2, ntiles(s) * P, 4], BF16, tag="xg", name="xg", align_bytes=64)
                st[("xg", s)] = xg
            xg32 = st[("xg", s)][:].bitcast(F32)
            g, h = banks(s)[b]
            psum_copy(
                copy_engine_x(s, b),
                xg32[:, g, h * 256 : (h + 1) * 256, :],
                st[("xt", s, b)][:].rearrange("p u j c -> p (j c) u"),
            )

        def quant_x(s):
            if not valid(s):
                return
            n = ntiles(s) * P
            xc = xq.tile([P, 2, n], U32, tag="xc", name="xc", align_bytes=256)
            xsc = xq.tile([P, 2, n], U8, tag="xsc", name="xsc", align_bytes=256)
            nc.vector.quantize_mx(
                out=xc[:].rearrange("p g n -> p (g n)").bitcast(FP8X4),
                scales=xsc[:].rearrange("p g n -> p (g n)"),
                in_=st[("xg", s)][:].rearrange("p g n t -> p (g n t)"),
            )
            st[("xc", s)] = xc
            st[("xsc", s)] = xsc

        def nb_pe(s):
            if not valid(s):
                return
            nt = ntiles(s)
            nbp = ps_n.tile([P, nt, P], F32, tag="nbp", name="nbp")
            for j in range(nt):
                nc.tensor.transpose(nbp[:, j, :], norm_col(s, j).to_broadcast([P, P]), ident[:])
            st[("nbp", s)] = nbp

        def nb_copy(s):
            if not valid(s):
                return
            nt = ntiles(s)
            nb = nbpool.tile([P, nt * P], F32, tag="nb", name="nb")
            psum_copy(copy_engine_nb(s), nb[:], st[("nbp", s)][:].rearrange("p j c -> p (j c)"))
            st[("nb", s)] = nb

        def mx1(s, t):
            if not valid(s):
                return
            n = ntiles(s) * P
            d = ps_d.tile([P, n], F32, tag="d", name="d")
            for g in range(2):
                nc.tensor.matmul_mx(
                    out=d[:],
                    lhsT=gc[:, g, t * P : (t + 1) * P].bitcast(FP8X4),
                    lhsT_scale=gsc[:, g, t * P : (t + 1) * P],
                    rhs=st[("xc", s)][:, g, :].bitcast(FP8X4),
                    rhs_scale=st[("xsc", s)][:, g, :],
                    start=(g == 0),
                    stop=(g == 1),
                )
            st[("d", s, t)] = d

        def cols(s, half):
            n = ntiles(s) * P
            return slice(0, n) if half is None else slice(half * n // 2, (half + 1) * n // 2)

        def stt(s, t, half=None):
            if not valid(s):
                return
            n = ntiles(s) * P
            c = cols(s, half)
            if ("z", s) not in st:
                z = work.tile([P, 4, n], F32, tag="z", name="z")
                st[("z", s)] = z
            nc.vector.scalar_tensor_tensor(
                out=st[("z", s)][:, t, c],
                in0=st[("nb", s)][:, c],
                scalar=nega[:, t : t + 1],
                in1=st[("d", s, t)][:, c],
                op0=ALU.mult,
                op1=ALU.add,
            )

        def expo(s, t, half=None):
            if not valid(s):
                return
            n = ntiles(s) * P
            c = cols(s, half)
            if ("f", s) not in st:
                f = work.tile([P, 4, n], BF16, tag="f", name="f")
                st[("f", s)] = f
            nc.scalar.activation(
                out=st[("f", s)][:, t, c],
                in_=st[("z", s)][:, t, c],
                func=ACT.Exp,
                bias=bias[:, t : t + 1],
                scale=1.0,
            )

        def regroup(s, half=None):
            if not valid(s):
                return
            n = ntiles(s) * P
            c = cols(s, half)
            if ("fg", s) not in st:
                if s >= NG - 2:
                    fg = work.tile([P, n, 4], BF16, tag="fgt", name="fg", align_bytes=64)
                else:
                    fg = single.tile([P, n, 4], BF16, tag="fg", name="fg", align_bytes=64)
                st[("fg", s)] = fg
            fg = st[("fg", s)]
            if regroup_engine(s) == "v":
                nc.vector.tensor_copy(
                    out=fg[:, c, :].rearrange("p (c i) t -> p c t i", i=4),
                    in_=st[("f", s)][:, :, c].rearrange("p t (c i) -> p c t i", i=4),
                )
            else:
                nc.gpsimd.tensor_scalar(
                    out=fg[:, c, :],
                    in0=st[("f", s)][:, :, c].rearrange("p t n -> p n t"),
                    scalar1=1.0,
                    scalar2=0.0,
                    op0=ALU.mult,
                    op1=ALU.add,
                )

        def quant_f(s, half=None):
            if not valid(s):
                return
            n = ntiles(s) * P
            c = cols(s, half)
            if s == 0:
                fc = wc
                fsc = wsc
            elif ("fc", s) in st:
                fc = st[("fc", s)]
                fsc = st[("fsc", s)]
            else:
                fc = work.tile([P, n], U32, tag="fc", name="fc", align_bytes=256)
                fsc = work.tile([P, n], U8, tag="fsc", name="fsc", align_bytes=256)
            nc.vector.quantize_mx(
                out=fc[:, c].bitcast(FP8X4),
                scales=fsc[:, c],
                in_=st[("fg", s)][:, c, :].rearrange("p n t -> p (n t)"),
            )
            st[("fc", s)] = fc
            st[("fsc", s)] = fsc

        def mx2(s, h):
            if not (1 <= s < NG):
                return
            if s >= TAIL_FROM:
                o = ps_d.tile([P, 2, O], F32, tag="d", name="o")
            else:
                o = ps_o.tile([P, 2, O], F32, tag="o", name="o")
            for jj in range(2):
                j = 2 * h + jj
                nc.tensor.matmul_mx(
                    out=o[:, jj, :],
                    lhsT=st[("fc", s)][:, j * P : (j + 1) * P].bitcast(FP8X4),
                    lhsT_scale=st[("fsc", s)][:, j * P : (j + 1) * P],
                    rhs=wc[:].bitcast(FP8X4),
                    rhs_scale=wsc[:],
                    start=True,
                    stop=True,
                )
            st[("o", s, h)] = o

        def out_copy(s, h):
            if not (1 <= s < NG):
                return
            if h == 0:
                osb = opool.tile([P, 4, O], F32, tag="osb", name="osb")
                st[("osb", s)] = osb
            osb = st[("osb", s)]
            psum_copy(copy_engine_out(s, h), osb[:, 2 * h : 2 * h + 2, :], st[("o", s, h)][:])
            dst = of[(s - 1) * GROUP : s * GROUP, :].rearrange("(p j) o -> p j o", j=4)
            if s >= TAIL_FROM - 1:
                nc.sync.dma_start(out=dst[:, 2 * h : 2 * h + 2, :], in_=osb[:, 2 * h : 2 * h + 2, :])
            elif h == 1:
                nc.sync.dma_start(out=dst, in_=osb[:])

        xt(0, [0, 1])
        norm(0, 0)
        norm(0, 1)
        xo(0, 0)
        xo(0, 1)
        xt(1, [0, 1])
        g_multiply(0)
        quant_x(0)
        g_multiply(1)
        norm(1, 0)
        norm(1, 1)
        xo(1, 0)
        g_multiply(2)
        g_multiply(3)
        xo(1, 1)
        g_transposes(0, 0)
        g_transposes(0, 1)
        nb_pe(0)
        g_out(0, 0)
        g_out(0, 1)
        g_transposes(1, 0)
        g_transposes(1, 1)
        xt(1, [2, 3])
        load(4)
        xo(1, 2)
        xo(1, 3)
        g_out(1, 0)
        g_out(1, 1)
        nb_copy(0)
        norm(1, 2)
        norm(1, 3)
        quant_g()
        load(5)
        xt(2, [0, 1])
        norm(2, 2)
        for t in range(3):
            mx1(0, t)
        quant_x(1)
        xo(2, 0)
        xo(2, 1)
        nb_pe(1)
        nb_copy(1)
        norm(2, 3)
        norm(2, 1)
        xt(2, [2, 3])
        load(6)

        for i in range(0, NG - 3):
            gram(i + 2)
            stt(i, 0)
            expo(i - 1, 3)
            stt(i, 1)
            mx1(i, 3)
            xo(i + 2, 2)
            xo(i + 2, 3)
            expo(i, 0)
            norm(i + 3, 2)
            mx1(i + 1, 0)
            mx2(i - 3, 1)
            stt(i, 2)
            quant_x(i + 2)
            diag(i + 2, 0)
            diag(i + 2, 1)
            xt(i + 3, [0, 1])
            nb_pe(i + 2)
            out_copy(i - 3, 1)
            expo(i, 1)
            quant_f(i - 2)
            nb_copy(i + 2)
            regroup(i - 1)
            load(i + 7)
            stt(i, 3)
            xo(i + 3, 0)
            norm(i + 3, 3)
            norm(i + 3, 1)
            xo(i + 3, 1)
            mx1(i + 1, 1)
            mx1(i + 1, 2)
            mx2(i - 2, 0)
            expo(i, 2)
            out_copy(i - 2, 0)
            xt(i + 3, [2, 3])

        gram(16)
        stt(14, 0)
        expo(13, 3)
        stt(14, 1)
        expo(14, 0)
        mx1(14, 3)
        xo(16, 3)
        xo(16, 2)
        expo(14, 1)
        mx1(15, 0)
        diag(16, 0)
        diag(16, 1)
        quant_f(12)
        quant_x(16)
        regroup(13)
        nb_pe(16)
        mx2(11, 1)
        stt(14, 2)
        expo(14, 2)
        nb_copy(16)
        mx1(15, 1)
        stt(14, 3)
        out_copy(11, 1)
        mx1(15, 2)
        expo(14, 3)
        stt(15, 0)
        mx1(15, 3)
        stt(15, 1)
        mx2(12, 0)
        mx1(16, 0)
        stt(15, 2)
        expo(15, 0)
        out_copy(12, 0)
        expo(15, 1)
        stt(15, 3)
        mx1(16, 1)
        mx1(16, 2)
        quant_f(13)
        regroup(14)
        expo(15, 2)
        expo(15, 3)
        mx1(16, 3)
        mx2(12, 1)
        out_copy(12, 1)
        for t in range(4):
            stt(16, t)
        mx2(13, 0)
        mx2(13, 1)
        out_copy(13, 0)
        regroup(15)
        for t in range(4):
            expo(16, t)
        quant_f(14)
        quant_f(15)
        out_copy(13, 1)
        mx2(14, 0)
        mx2(14, 1)
        regroup(16, 0)
        regroup(16, 1)
        out_copy(14, 0)
        out_copy(14, 1)
        mx2(15, 0)
        mx2(15, 1)
        out_copy(15, 0)
        quant_f(16, 0)
        quant_f(16, 1)
        out_copy(15, 1)
        mx2(16, 0)
        mx2(16, 1)
        out_copy(16, 0)
        out_copy(16, 1)
